import numpy as np
import ml_dtypes


def mxq(x, axis, fmt="e4m3"):
    dtype, down = {"e4m3": (ml_dtypes.float8_e4m3fn, 7), "e5m2": (ml_dtypes.float8_e5m2, 14)}[fmt]
    v = np.moveaxis(np.asarray(x, np.float32).astype(ml_dtypes.bfloat16).astype(np.float64), axis, -1)
    blocks = v.reshape(v.shape[:-1] + (-1, 32))
    amax = np.abs(blocks).max(-1, keepdims=True)
    byte = np.maximum(np.where(amax > 0, np.frexp(amax)[1] - 1 + 127, 0) - down, 1)
    scale = np.exp2(byte - 127.0)
    codes = (blocks / scale).astype(np.float32).astype(dtype).astype(np.float64)
    return np.moveaxis((codes * scale).reshape(v.shape), -1, axis)


WIDE = False


def mx_kscale(k):
    if not WIDE:
        return np.ones(k)
    levels = np.array([10, -10, 5, -5, 0])
    if k % 512:
        return np.exp2(np.random.permutation(np.resize(levels, k // 32))).repeat(32)
    a = np.empty((k // 512, 16))
    for p in range(k // 512):
        a[p, :8] = np.random.permutation(np.resize(levels, 8))
        for g in range(8):
            far = levels[np.abs(levels - a[p, g]) >= 10]
            a[p, g + 8] = far[np.random.randint(len(far))]
    return np.exp2(a.ravel()).repeat(32)


BF16 = ml_dtypes.bfloat16


def bf(x):
    return np.asarray(x, np.float32).astype(BF16)


def f64(x):
    return np.asarray(x).astype(np.float64)


B, S, HID, H, HKV, DH = 2, 128, 2048, 16, 16, 128
NH = H + 2 * HKV


def rotate_half(x):
    x1 = x[..., ::2]
    x2 = x[..., 1::2]
    return np.stack((-x2, x1), axis=-1).reshape(x.shape)


def setup_inputs():
    s = mx_kscale(HID)
    inv_freq = 1.0 / (10000.0 ** (np.arange(0, DH, 2) / DH))
    emb = np.repeat(np.outer(np.arange(S), inv_freq), 2, axis=-1)
    return {"hidden_states": bf(np.random.standard_normal((B, S, HID)) * s),
            "cos": bf(np.cos(emb)),
            "sin": bf(np.sin(emb)),
            "w_qkv": bf(np.random.standard_normal((NH * DH, HID)) / np.sqrt(HID) / s[None, :])}


def reference(hidden_states, cos, sin, w_qkv):
    qkv = mxq(f64(hidden_states), 2, "e4m3") @ mxq(f64(w_qkv), 1, "e4m3").T
    qkv = qkv.reshape(B, S, NH, DH)
    q = qkv[:, :, :H]
    k = qkv[:, :, H:H + HKV]
    v = qkv[:, :, H + HKV:]
    cos_s = f64(cos)[:S][None, :, None, :]
    sin_s = f64(sin)[:S][None, :, None, :]
    q = q * cos_s + rotate_half(q) * sin_s
    k = k * cos_s + rotate_half(k) * sin_s
    return q, k, v

@@ -1,0 +1,190 @@
+from contextlib import ExitStack
+
+import concourse.mybir as mybir
+from concourse.masks import make_identity
+
+F32 = mybir.dt.float32
+BF16 = mybir.dt.bfloat16
+U32 = mybir.dt.uint32
+U8 = mybir.dt.uint8
+FP8X4 = mybir.dt.float8_e4m3fn_x4
+MULT = mybir.AluOpType.mult
+ADD = mybir.AluOpType.add
+
+FLOPS = 2 * 256 * 6144 * 2048
+
+P = 128
+NUNIT = 24
+W_BUFS = 12
+GRP_BUFS = 4
+CODE_BUFS = 4
+OST_BUFS = 10
+T_BANKS = 4
+A_BANKS = 4
+R_BUFS = 3
+PATTERN = "RRRVRRRVRRVV"
+GADD = True
+PLAIN_ENG = "v"
+LAG = 2
+STORE_Q = "sync"
+
+
+def tile_attention_pa_kernel(tc, hidden_states, cos, sin, w_qkv, out_0, out_1, out_2):
+    nc = tc.nc
+    outs = (out_0, out_1, out_2)
+    rotated = [(kind, hc) for hc in range(4) for kind in range(2)]
+    plain = [(2, hc) for hc in range(4)]
+    groups = []
+    for ch in PATTERN:
+        groups.append(rotated.pop(0) if ch == "R" else plain.pop(0))
+    with ExitStack() as ctx:
+        const = ctx.enter_context(tc.tile_pool(name="const", bufs=1))
+        wpool = ctx.enter_context(tc.tile_pool(name="wpool", bufs=W_BUFS))
+        gpool = ctx.enter_context(tc.tile_pool(name="gpool", bufs=GRP_BUFS))
+        cpool = ctx.enter_context(tc.tile_pool(name="cpool", bufs=CODE_BUFS))
+        rpool = ctx.enter_context(tc.tile_pool(name="rpool", bufs=R_BUFS))
+        opool = ctx.enter_context(tc.tile_pool(name="opool", bufs=OST_BUFS))
+        psum_t = ctx.enter_context(tc.psum_pool(name="psum_t", bufs=T_BANKS))
+        psum_a = ctx.enter_context(tc.psum_pool(name="psum_a", bufs=A_BANKS))
+        ctx.enter_context(tc.manual_schedule())
+        store_eng = {"sync": nc.sync, "gpsimd": nc.gpsimd, "scalar": nc.scalar}[STORE_Q]
+
+        ident = const.tile([P, P], F32)
+        make_identity(nc, ident[:])
+        cos_raw = const.tile([P, P], BF16)
+        sin_raw = const.tile([P, P], BF16)
+        nc.scalar.dma_start(out=cos_raw[:], in_=cos)
+        nc.scalar.dma_start(out=sin_raw[:], in_=sin)
+
+        xraw = const.tile([P, 4096], BF16)
+        x_dram = hidden_states.rearrange("b s k -> s b k")
+        x_sb = xraw[:].rearrange("p (b k) -> p b k", b=2)
+        for hf in range(2):
+            nc.sync.dma_start(out=x_sb[:, :, 1024 * hf:1024 * hf + 1024],
+                              in_=x_dram[:, :, 1024 * hf:1024 * hf + 1024])
+
+        wraws = []
+        for u in range(NUNIT):
+            kind, hc = groups[u // 2]
+            r0 = 2048 * kind + 512 * hc + 256 * (u % 2)
+            wraw = wpool.tile([P, 4096], BF16)
+            wraws.append(wraw)
+            nc.sync.dma_start(out=wraw[:].rearrange("p (j k) -> p j k", j=2),
+                              in_=w_qkv[r0:r0 + 256, :].rearrange("(j p) k -> p j k", j=2))
+
+        xf = xraw[:].bitcast(F32)
+        xgrp = const.tile([P, 4096], BF16, align_bytes=64)
+        xgf = xgrp[:].bitcast(F32)
+        xc = const.tile([P, 1024], U32, align_bytes=64)
+        xs = const.tile([P, 1024], U8, align_bytes=64)
+        for g in range(4):
+            tpx = psum_t.tile([P, 512], F32, tag="tp")
+            for t in range(4):
+                o = 1024 * (t // 2) + 256 * g
+                nc.tensor.transpose(tpx[:, 128 * t:128 * t + 128], xf[:, o + t % 2:o + 256:2], ident[:])
+            dst = xgf[:, 512 * g:512 * g + 512].rearrange("q (b s u) -> q b s u", b=2, u=2)
+            src = tpx[:].rearrange("q (b u s) -> q b s u", b=2, u=2)
+            if g % 2 == 0:
+                nc.scalar.copy(out=dst, in_=src)
+            else:
+                nc.vector.tensor_copy(out=dst, in_=src)
+        for hf in range(2):
+            nc.vector.quantize_mx(out=xc[:, 512 * hf:512 * hf + 512].bitcast(FP8X4),
+                                  scales=xs[:, 512 * hf:512 * hf + 512],
+                                  in_=xgrp[:, 2048 * hf:2048 * hf + 2048])
+
+        cosd = const.tile([P, P], F32)
+        sind = const.tile([P, P], F32)
+        nc.vector.tensor_copy(out=cosd[:], in_=cos_raw[:])
+        sin_v = sin_raw[:].rearrange("p (i e) -> p i e", e=2)
+        sind_v = sind[:].rearrange("p (i e) -> p i e", e=2)
+        nc.vector.tensor_scalar_mul(out=sind_v[:, :, 0], in0=sin_v[:, :, 0], scalar1=-1.0)
+        nc.vector.tensor_copy(out=sind_v[:, :, 1], in_=sin_v[:, :, 1])
+
+        grps = {}
+        codes = {}
+        accs = {}
+        osts = {}
+
+        def transposes(u):
+            wf = wraws[u][:].bitcast(F32)
+            grp = gpool.tile([P, 4096], BF16, align_bytes=64, tag="grp")
+            grps[u] = grp
+            gf = grp[:].bitcast(F32)
+            for g in range(4):
+                tp = psum_t.tile([P, 512], F32, tag="tp")
+                for t in range(4):
+                    o = 1024 * (t // 2) + 256 * g
+                    nc.tensor.transpose(tp[:, 128 * t:128 * t + 128], wf[:, o + t % 2:o + 256:2], ident[:])
+                nc.scalar.copy(out=gf[:, 512 * g:512 * g + 512].rearrange("q (j c u) -> q j c u", j=2, u=2),
+                               in_=tp[:].rearrange("q (j u c) -> q j c u", j=2, u=2))
+
+        def quantise(u):
+            wc = cpool.tile([P, 1024], U32, align_bytes=64, tag="wc")
+            ws = cpool.tile([P, 1024], U8, align_bytes=64, tag="ws")
+            codes[u] = (wc, ws)
+            pieces = 4 if u == NUNIT - 1 else 1
+            n = 1024 // pieces
+            for i in range(pieces):
+                nc.vector.quantize_mx(out=wc[:, n * i:n * i + n].bitcast(FP8X4), scales=ws[:, n * i:n * i + n],
+                                      in_=grps[u][:, 4 * n * i:4 * n * i + 4 * n])
+
+        def matmuls(u):
+            acc = psum_a.tile([P, 512], F32, tag="acc")
+            accs[u] = acc
+            wc, ws = codes[u]
+            for b in range(2):
+                for g in range(4):
+                    xo = 256 * g + 128 * b
+                    nc.tensor.matmul_mx(out=acc[:, 256 * b:256 * b + 256],
+                                        lhsT=xc[:, xo:xo + 128].bitcast(FP8X4), lhsT_scale=xs[:, xo:xo + 128],
+                                        rhs=wc[:, 256 * g:256 * g + 256].bitcast(FP8X4),
+                                        rhs_scale=ws[:, 256 * g:256 * g + 256],
+                                        start=(g == 0), stop=(g == 3))
+
+        def finish(u):
+            kind, hc = groups[u // 2]
+            jp = u % 2
+            acc = accs[u]
+            if jp == 0:
+                ost = opool.tile([P, 1024], F32, tag="ost")
+                osts[u // 2] = ost
+            ost = osts[u // 2]
+            dst = ost[:].rearrange("p (b m) -> p b m", b=2)[:, :, 256 * jp:256 * jp + 256]
+            if kind < 2:
+                t1 = rpool.tile([P, 512], F32, tag="t1")
+                t2 = rpool.tile([P, 512], F32, tag="t2")
+                nc.vector.tensor_tensor(out=t1[:].rearrange("p (h m) -> p h m", h=4),
+                                        in0=acc[:].rearrange("p (h m) -> p h m", h=4),
+                                        in1=cosd[:].unsqueeze(1).to_broadcast([P, 4, P]), op=MULT)
+                nc.vector.tensor_tensor(
+                    out=t2[:].rearrange("p (h i e) -> p h i e", h=4, e=2),
+                    in0=acc[:].rearrange("p (h i e) -> p h i e", h=4, e=2)[:, :, :, ::-1],
+                    in1=sind[:].rearrange("p (i e) -> p i e", e=2).unsqueeze(1).to_broadcast([P, 4, 64, 2]),
+                    op=MULT)
+                add_eng = nc.gpsimd if GADD else nc.vector
+                add_eng.tensor_tensor(out=dst, in0=t1[:].rearrange("p (b m) -> p b m", b=2),
+                                      in1=t2[:].rearrange("p (b m) -> p b m", b=2), op=ADD)
+            else:
+                src = acc[:].rearrange("p (b m) -> p b m", b=2)
+                if PLAIN_ENG == "s" or u >= NUNIT - 2:
+                    nc.scalar.copy(out=dst, in_=src)
+                else:
+                    nc.vector.tensor_copy(out=dst, in_=src)
+            o_dram = outs[kind].rearrange("b s h l -> s b (h l)")
+            if u // 2 == NUNIT // 2 - 1:
+                lo = 512 * hc + 256 * jp
+                store_eng.dma_start(out=o_dram[:, :, lo:lo + 256], in_=dst)
+            elif jp == 1:
+                store_eng.dma_start(out=o_dram[:, :, 512 * hc:512 * hc + 512],
+                                    in_=ost[:].rearrange("p (b m) -> p b m", b=2))
+
+        for u in range(NUNIT + LAG):
+            if u < NUNIT:
+                transposes(u)
+            if u >= LAG:
+                matmuls(u - LAG)
+            if u < NUNIT:
+                quantise(u)
+            if u >= LAG:
+                finish(u - LAG)

@@ -16,16 +16,17 @@ FLOPS = 2 * 256 * 6144 * 2048
 P = 128
 NUNIT = 24
 W_BUFS = 12
-GRP_BUFS = 4
-CODE_BUFS = 4
+GRP_BUFS = 3
+CODE_BUFS = 3
+EVEN_BUFS = 3
+SPLIT = {"R": 4, "V": 8}
 OST_BUFS = 10
 T_BANKS = 4
 A_BANKS = 4
 R_BUFS = 3
-PATTERN = "RRRVRRRVRRVV"
+PATTERN = "RRVRRVRRVRRV"
 GADD = True
-PLAIN_ENG = "v"
-LAG = 2
+PLAIN_ENG = "s"
 STORE_Q = "sync"
 
 
@@ -40,6 +41,7 @@ def tile_attention_pa_kernel(tc, hidden_states, cos, sin, w_qkv, out_0, out_1, o
     with ExitStack() as ctx:
         const = ctx.enter_context(tc.tile_pool(name="const", bufs=1))
         wpool = ctx.enter_context(tc.tile_pool(name="wpool", bufs=W_BUFS))
+        epool = ctx.enter_context(tc.tile_pool(name="epool", bufs=EVEN_BUFS))
         gpool = ctx.enter_context(tc.tile_pool(name="gpool", bufs=GRP_BUFS))
         cpool = ctx.enter_context(tc.tile_pool(name="cpool", bufs=CODE_BUFS))
         rpool = ctx.enter_context(tc.tile_pool(name="rpool", bufs=R_BUFS))
@@ -101,10 +103,22 @@ def tile_attention_pa_kernel(tc, hidden_states, cos, sin, w_qkv, out_0, out_1, o
         nc.vector.tensor_scalar_mul(out=sind_v[:, :, 0], in0=sin_v[:, :, 0], scalar1=-1.0)
         nc.vector.tensor_copy(out=sind_v[:, :, 1], in_=sin_v[:, :, 1])
 
+        splits = {}
         grps = {}
         codes = {}
         accs = {}
         osts = {}
+
+        def split_blocks(u):
+            return 0 if u == 0 else SPLIT[PATTERN[u // 2]]
+
+        def split_words(u):
+            n = split_blocks(u)
+            wf = wraws[u][:].bitcast(F32)
+            split = epool.tile([P, 2048], F32, tag="split")
+            splits[u] = split
+            nc.vector.tensor_copy(out=split[:, 0:256 * n].rearrange("p (m u q) -> p m u q", m=n, u=2),
+                                  in_=wf[:, 0:256 * n].rearrange("p (m q u) -> p m u q", m=n, u=2))
 
         def transposes(u):
             wf = wraws[u][:].bitcast(F32)
@@ -113,9 +127,15 @@ def tile_attention_pa_kernel(tc, hidden_states, cos, sin, w_qkv, out_0, out_1, o
             gf = grp[:].bitcast(F32)
             for g in range(4):
                 tp = psum_t.tile([P, 512], F32, tag="tp")
-                for t in range(4):
-                    o = 1024 * (t // 2) + 256 * g
-                    nc.tensor.transpose(tp[:, 128 * t:128 * t + 128], wf[:, o + t % 2:o + 256:2], ident[:])
+                for j in range(2):
+                    m = 4 * j + g
+                    for t in range(2):
+                        if m < split_blocks(u):
+                            in_ = splits[u][:, 256 * m + 128 * t:256 * m + 128 * t + 128]
+                        else:
+                            in_ = wf[:, 256 * m + t:256 * m + 256:2]
+                        o = 256 * j + 128 * t
+                        nc.tensor.transpose(tp[:, o:o + 128], in_, ident[:])
                 nc.scalar.copy(out=gf[:, 512 * g:512 * g + 512].rearrange("q (j c u) -> q j c u", j=2, u=2),
                                in_=tp[:].rearrange("q (j u c) -> q j c u", j=2, u=2))
 
@@ -179,12 +199,14 @@ def tile_attention_pa_kernel(tc, hidden_states, cos, sin, w_qkv, out_0, out_1, o
                 store_eng.dma_start(out=o_dram[:, :, 512 * hc:512 * hc + 512],
                                     in_=ost[:].rearrange("p (b m) -> p b m", b=2))
 
-        for u in range(NUNIT + LAG):
+        for u in range(NUNIT + 2):
             if u < NUNIT:
                 transposes(u)
-            if u >= LAG:
-                matmuls(u - LAG)
-            if u < NUNIT:
-                quantise(u)
-            if u >= LAG:
-                finish(u - LAG)
+            if u >= 2:
+                matmuls(u - 2)
+            if u + 1 < NUNIT:
+                split_words(u + 1)
+            if 1 <= u < NUNIT + 1:
+                quantise(u - 1)
+            if u >= 2:
+                finish(u - 2)

@@ -15,19 +15,14 @@ FLOPS = 2 * 256 * 6144 * 2048
 
 P = 128
 NUNIT = 24
-W_BUFS = 12
+PATTERN = "RRVRRVRRVRRV"
+W_BUFS = 10
+SPLIT_BUFS = 3
 GRP_BUFS = 3
 CODE_BUFS = 3
-EVEN_BUFS = 3
-SPLIT = {"R": 4, "V": 8}
-OST_BUFS = 10
-T_BANKS = 4
-A_BANKS = 4
-R_BUFS = 3
-PATTERN = "RRVRRVRRVRRV"
-GADD = True
-PLAIN_ENG = "s"
-STORE_Q = "sync"
+ROT_BUFS = 3
+OUT_BUFS = 8
+SCALAR_CHUNKS = 24
 
 
 def tile_attention_pa_kernel(tc, hidden_states, cos, sin, w_qkv, out_0, out_1, out_2):
@@ -41,29 +36,26 @@ def tile_attention_pa_kernel(tc, hidden_states, cos, sin, w_qkv, out_0, out_1, o
     with ExitStack() as ctx:
         const = ctx.enter_context(tc.tile_pool(name="const", bufs=1))
         wpool = ctx.enter_context(tc.tile_pool(name="wpool", bufs=W_BUFS))
-        epool = ctx.enter_context(tc.tile_pool(name="epool", bufs=EVEN_BUFS))
+        spool = ctx.enter_context(tc.tile_pool(name="spool", bufs=SPLIT_BUFS))
         gpool = ctx.enter_context(tc.tile_pool(name="gpool", bufs=GRP_BUFS))
         cpool = ctx.enter_context(tc.tile_pool(name="cpool", bufs=CODE_BUFS))
-        rpool = ctx.enter_context(tc.tile_pool(name="rpool", bufs=R_BUFS))
-        opool = ctx.enter_context(tc.tile_pool(name="opool", bufs=OST_BUFS))
-        psum_t = ctx.enter_context(tc.psum_pool(name="psum_t", bufs=T_BANKS))
-        psum_a = ctx.enter_context(tc.psum_pool(name="psum_a", bufs=A_BANKS))
+        rpool = ctx.enter_context(tc.tile_pool(name="rpool", bufs=ROT_BUFS))
+        opool = ctx.enter_context(tc.tile_pool(name="opool", bufs=OUT_BUFS))
+        psum_t = ctx.enter_context(tc.psum_pool(name="psum_t", bufs=4))
+        psum_a = ctx.enter_context(tc.psum_pool(name="psum_a", bufs=4))
         ctx.enter_context(tc.manual_schedule())
-        store_eng = {"sync": nc.sync, "gpsimd": nc.gpsimd, "scalar": nc.scalar}[STORE_Q]
 
         ident = const.tile([P, P], F32)
         make_identity(nc, ident[:])
+        xraw = const.tile([P, 4096], BF16)
+        x_dram = hidden_states.rearrange("b s k -> s b k")
+        x_sb = xraw[:].rearrange("p (b k) -> p b k", b=2)
+        for g in range(4):
+            nc.sync.dma_start(out=x_sb[:, :, 512 * g:512 * g + 512], in_=x_dram[:, :, 512 * g:512 * g + 512])
         cos_raw = const.tile([P, P], BF16)
         sin_raw = const.tile([P, P], BF16)
         nc.scalar.dma_start(out=cos_raw[:], in_=cos)
         nc.scalar.dma_start(out=sin_raw[:], in_=sin)
-
-        xraw = const.tile([P, 4096], BF16)
-        x_dram = hidden_states.rearrange("b s k -> s b k")
-        x_sb = xraw[:].rearrange("p (b k) -> p b k", b=2)
-        for hf in range(2):
-            nc.sync.dma_start(out=x_sb[:, :, 1024 * hf:1024 * hf + 1024],
-                              in_=x_dram[:, :, 1024 * hf:1024 * hf + 1024])
 
         wraws = []
         for u in range(NUNIT):
@@ -71,37 +63,39 @@ def tile_attention_pa_kernel(tc, hidden_states, cos, sin, w_qkv, out_0, out_1, o
             r0 = 2048 * kind + 512 * hc + 256 * (u % 2)
             wraw = wpool.tile([P, 4096], BF16)
             wraws.append(wraw)
-            nc.sync.dma_start(out=wraw[:].rearrange("p (j k) -> p j k", j=2),
-                              in_=w_qkv[r0:r0 + 256, :].rearrange("(j p) k -> p j k", j=2))
+            w_sb = wraw[:].rearrange("p (j k) -> p j k", j=2)
+            w_dram = w_qkv[r0:r0 + 256, :].rearrange("(j p) k -> p j k", j=2)
+            step = 1024 if u == 0 else 2048
+            for k0 in range(0, 2048, step):
+                nc.sync.dma_start(out=w_sb[:, :, k0:k0 + step], in_=w_dram[:, :, k0:k0 + step])
 
         xf = xraw[:].bitcast(F32)
+        xsplit = const.tile([P, 2048], F32)
         xgrp = const.tile([P, 4096], BF16, align_bytes=64)
         xgf = xgrp[:].bitcast(F32)
         xc = const.tile([P, 1024], U32, align_bytes=64)
         xs = const.tile([P, 1024], U8, align_bytes=64)
         for g in range(4):
+            nc.vector.tensor_copy(
+                out=xsplit[:, 512 * g:512 * g + 512].rearrange("p (u b c w) -> p u b c w", u=2, b=2, c=16),
+                in_=xf.rearrange("p (b g c u w) -> p g u b c w", b=2, g=4, c=16, u=2)[:, g])
+        for g in range(4):
             tpx = psum_t.tile([P, 512], F32, tag="tp")
-            for t in range(4):
-                o = 1024 * (t // 2) + 256 * g
-                nc.tensor.transpose(tpx[:, 128 * t:128 * t + 128], xf[:, o + t % 2:o + 256:2], ident[:])
-            dst = xgf[:, 512 * g:512 * g + 512].rearrange("q (b s u) -> q b s u", b=2, u=2)
-            src = tpx[:].rearrange("q (b u s) -> q b s u", b=2, u=2)
-            if g % 2 == 0:
-                nc.scalar.copy(out=dst, in_=src)
-            else:
-                nc.vector.tensor_copy(out=dst, in_=src)
-        for hf in range(2):
-            nc.vector.quantize_mx(out=xc[:, 512 * hf:512 * hf + 512].bitcast(FP8X4),
-                                  scales=xs[:, 512 * hf:512 * hf + 512],
-                                  in_=xgrp[:, 2048 * hf:2048 * hf + 2048])
+            for u in range(2):
+                for b in range(2):
+                    i = 512 * g + 256 * u + 128 * b
+                    o = 256 * b + 128 * u
+                    nc.tensor.transpose(tpx[:, o:o + 128], xsplit[:, i:i + 128], ident[:])
+            nc.scalar.copy(out=xgf[:, 512 * g:512 * g + 512].rearrange("q (b s u) -> q b s u", b=2, u=2),
+                           in_=tpx[:].rearrange("q (b u s) -> q b s u", b=2, u=2))
 
         cosd = const.tile([P, P], F32)
         sind = const.tile([P, P], F32)
-        nc.vector.tensor_copy(out=cosd[:], in_=cos_raw[:])
+        nc.gpsimd.tensor_copy(out=cosd[:], in_=cos_raw[:])
         sin_v = sin_raw[:].rearrange("p (i e) -> p i e", e=2)
         sind_v = sind[:].rearrange("p (i e) -> p i e", e=2)
-        nc.vector.tensor_scalar_mul(out=sind_v[:, :, 0], in0=sin_v[:, :, 0], scalar1=-1.0)
-        nc.vector.tensor_copy(out=sind_v[:, :, 1], in_=sin_v[:, :, 1])
+        nc.gpsimd.tensor_scalar(out=sind_v[:, :, 0], in0=sin_v[:, :, 0], scalar1=-1.0, scalar2=None, op0=MULT)
+        nc.gpsimd.tensor_copy(out=sind_v[:, :, 1], in_=sin_v[:, :, 1])
 
         splits = {}
         grps = {}
@@ -109,33 +103,34 @@ def tile_attention_pa_kernel(tc, hidden_states, cos, sin, w_qkv, out_0, out_1, o
         accs = {}
         osts = {}
 
-        def split_blocks(u):
-            return 0 if u == 0 else SPLIT[PATTERN[u // 2]]
+        def split_part(u, engine_copy, c0, c1):
+            src = wraws[u][:].bitcast(F32).rearrange("p (c u w) -> p u c w", u=2, w=8)
+            dst = splits[u][:].rearrange("p (u c w) -> p u c w", u=2, w=8)
+            engine_copy(out=dst[:, :, c0:c1, :], in_=src[:, :, c0:c1, :])
 
         def split_words(u):
-            n = split_blocks(u)
-            wf = wraws[u][:].bitcast(F32)
-            split = epool.tile([P, 2048], F32, tag="split")
+            split = spool.tile([P, 2048], F32, tag="split")
             splits[u] = split
-            nc.vector.tensor_copy(out=split[:, 0:256 * n].rearrange("p (m u q) -> p m u q", m=n, u=2),
-                                  in_=wf[:, 0:256 * n].rearrange("p (m q u) -> p m u q", m=n, u=2))
+            if u == 0:
+                for hf in range(2):
+                    for j in range(2):
+                        c0 = 64 * j + 32 * hf
+                        split_part(u, nc.vector.tensor_copy, c0, c0 + 32)
+            else:
+                split_part(u, nc.vector.tensor_copy, 0, 128 - SCALAR_CHUNKS)
+                split_part(u, nc.scalar.copy, 128 - SCALAR_CHUNKS, 128)
 
         def transposes(u):
-            wf = wraws[u][:].bitcast(F32)
             grp = gpool.tile([P, 4096], BF16, align_bytes=64, tag="grp")
             grps[u] = grp
             gf = grp[:].bitcast(F32)
             for g in range(4):
                 tp = psum_t.tile([P, 512], F32, tag="tp")
                 for j in range(2):
-                    m = 4 * j + g
-                    for t in range(2):
-                        if m < split_blocks(u):
-                            in_ = splits[u][:, 256 * m + 128 * t:256 * m + 128 * t + 128]
-                        else:
-                            in_ = wf[:, 256 * m + t:256 * m + 256:2]
-                        o = 256 * j + 128 * t
-                        nc.tensor.transpose(tp[:, o:o + 128], in_, ident[:])
+                    for h in range(2):
+                        i = 1024 * h + 512 * j + 128 * g
+                        o = 256 * j + 128 * h
+                        nc.tensor.transpose(tp[:, o:o + 128], splits[u][:, i:i + 128], ident[:])
                 nc.scalar.copy(out=gf[:, 512 * g:512 * g + 512].rearrange("q (j c u) -> q j c u", j=2, u=2),
                                in_=tp[:].rearrange("q (j u c) -> q j c u", j=2, u=2))
 
@@ -182,31 +177,31 @@ def tile_attention_pa_kernel(tc, hidden_states, cos, sin, w_qkv, out_0, out_1, o
                     in0=acc[:].rearrange("p (h i e) -> p h i e", h=4, e=2)[:, :, :, ::-1],
                     in1=sind[:].rearrange("p (i e) -> p i e", e=2).unsqueeze(1).to_broadcast([P, 4, 64, 2]),
                     op=MULT)
-                add_eng = nc.gpsimd if GADD else nc.vector
-                add_eng.tensor_tensor(out=dst, in0=t1[:].rearrange("p (b m) -> p b m", b=2),
-                                      in1=t2[:].rearrange("p (b m) -> p b m", b=2), op=ADD)
+                nc.gpsimd.tensor_tensor(out=dst, in0=t1[:].rearrange("p (b m) -> p b m", b=2),
+                                        in1=t2[:].rearrange("p (b m) -> p b m", b=2), op=ADD)
             else:
-                src = acc[:].rearrange("p (b m) -> p b m", b=2)
-                if PLAIN_ENG == "s" or u >= NUNIT - 2:
-                    nc.scalar.copy(out=dst, in_=src)
-                else:
-                    nc.vector.tensor_copy(out=dst, in_=src)
+                nc.scalar.copy(out=dst, in_=acc[:].rearrange("p (b m) -> p b m", b=2))
             o_dram = outs[kind].rearrange("b s h l -> s b (h l)")
             if u // 2 == NUNIT // 2 - 1:
                 lo = 512 * hc + 256 * jp
-                store_eng.dma_start(out=o_dram[:, :, lo:lo + 256], in_=dst)
+                nc.sync.dma_start(out=o_dram[:, :, lo:lo + 256], in_=dst)
             elif jp == 1:
-                store_eng.dma_start(out=o_dram[:, :, 512 * hc:512 * hc + 512],
-                                    in_=ost[:].rearrange("p (b m) -> p b m", b=2))
+                nc.sync.dma_start(out=o_dram[:, :, 512 * hc:512 * hc + 512],
+                                  in_=ost[:].rearrange("p (b m) -> p b m", b=2))
 
-        for u in range(NUNIT + 2):
-            if u < NUNIT:
-                transposes(u)
-            if u >= 2:
-                matmuls(u - 2)
+        split_words(0)
+        for hf in range(2):
+            nc.vector.quantize_mx(out=xc[:, 512 * hf:512 * hf + 512].bitcast(FP8X4),
+                                  scales=xs[:, 512 * hf:512 * hf + 512],
+                                  in_=xgrp[:, 2048 * hf:2048 * hf + 2048])
+        for u in range(NUNIT + 3):
             if u + 1 < NUNIT:
                 split_words(u + 1)
+            if u < NUNIT:
+                transposes(u)
+            if 2 <= u < NUNIT + 2:
+                matmuls(u - 2)
+            if u >= 3:
+                finish(u - 3)
             if 1 <= u < NUNIT + 1:
                 quantise(u - 1)
-            if u >= 2:
-                finish(u - 2)

@@ -16,13 +16,12 @@ FLOPS = 2 * 256 * 6144 * 2048
 P = 128
 NUNIT = 24
 PATTERN = "RRVRRVRRVRRV"
-W_BUFS = 10
-SPLIT_BUFS = 3
+W_BUFS = 11
+EVEN_BUFS = 4
 GRP_BUFS = 3
 CODE_BUFS = 3
 ROT_BUFS = 3
 OUT_BUFS = 8
-SCALAR_CHUNKS = 24
 
 
 def tile_attention_pa_kernel(tc, hidden_states, cos, sin, w_qkv, out_0, out_1, out_2):
@@ -36,7 +35,7 @@ def tile_attention_pa_kernel(tc, hidden_states, cos, sin, w_qkv, out_0, out_1, o
     with ExitStack() as ctx:
         const = ctx.enter_context(tc.tile_pool(name="const", bufs=1))
         wpool = ctx.enter_context(tc.tile_pool(name="wpool", bufs=W_BUFS))
-        spool = ctx.enter_context(tc.tile_pool(name="spool", bufs=SPLIT_BUFS))
+        epool = ctx.enter_context(tc.tile_pool(name="epool", bufs=EVEN_BUFS))
         gpool = ctx.enter_context(tc.tile_pool(name="gpool", bufs=GRP_BUFS))
         cpool = ctx.enter_context(tc.tile_pool(name="cpool", bufs=CODE_BUFS))
         rpool = ctx.enter_context(tc.tile_pool(name="rpool", bufs=ROT_BUFS))
@@ -50,8 +49,8 @@ def tile_attention_pa_kernel(tc, hidden_states, cos, sin, w_qkv, out_0, out_1, o
         xraw = const.tile([P, 4096], BF16)
         x_dram = hidden_states.rearrange("b s k -> s b k")
         x_sb = xraw[:].rearrange("p (b k) -> p b k", b=2)
-        for g in range(4):
-            nc.sync.dma_start(out=x_sb[:, :, 512 * g:512 * g + 512], in_=x_dram[:, :, 512 * g:512 * g + 512])
+        for k0 in range(0, 2048, 1024):
+            nc.sync.dma_start(out=x_sb[:, :, k0:k0 + 1024], in_=x_dram[:, :, k0:k0 + 1024])
         cos_raw = const.tile([P, P], BF16)
         sin_raw = const.tile([P, P], BF16)
         nc.scalar.dma_start(out=cos_raw[:], in_=cos)
@@ -69,23 +68,32 @@ def tile_attention_pa_kernel(tc, hidden_states, cos, sin, w_qkv, out_0, out_1, o
             for k0 in range(0, 2048, step):
                 nc.sync.dma_start(out=w_sb[:, :, k0:k0 + step], in_=w_dram[:, :, k0:k0 + step])
 
+        def gather_even(words, even, m0, m1):
+            nc.vector.tensor_copy(
+                out=even[:, 128 * m0:128 * m1].rearrange("p (m c s w) -> p m c s w", c=8, s=2, w=8),
+                in_=words[:, 256 * m0:256 * m1].rearrange("p (m s c v w) -> p v m c s w", s=2, c=8, v=2, w=8)[:, 0])
+
+        def move_odd(words, copy, m0, m1):
+            view = words[:, 256 * m0:256 * m1].rearrange("p (m s c v w) -> p s v m c w", s=2, c=8, v=2, w=8)
+            copy(out=view[:, 1, 0], in_=view[:, 0, 1])
+
         xf = xraw[:].bitcast(F32)
-        xsplit = const.tile([P, 2048], F32)
+        xeven = const.tile([P, 1024], F32)
         xgrp = const.tile([P, 4096], BF16, align_bytes=64)
         xgf = xgrp[:].bitcast(F32)
         xc = const.tile([P, 1024], U32, align_bytes=64)
         xs = const.tile([P, 1024], U8, align_bytes=64)
-        for g in range(4):
-            nc.vector.tensor_copy(
-                out=xsplit[:, 512 * g:512 * g + 512].rearrange("p (u b c w) -> p u b c w", u=2, b=2, c=16),
-                in_=xf.rearrange("p (b g c u w) -> p g u b c w", b=2, g=4, c=16, u=2)[:, g])
+        for hf in range(2):
+            for b in range(2):
+                m = 4 * b + 2 * hf
+                gather_even(xf, xeven, m, m + 2)
+                move_odd(xf, nc.scalar.copy, m, m + 2)
         for g in range(4):
             tpx = psum_t.tile([P, 512], F32, tag="tp")
-            for u in range(2):
-                for b in range(2):
-                    i = 512 * g + 256 * u + 128 * b
-                    o = 256 * b + 128 * u
-                    nc.tensor.transpose(tpx[:, o:o + 128], xsplit[:, i:i + 128], ident[:])
+            for b in range(2):
+                m = 4 * b + g
+                nc.tensor.transpose(tpx[:, 256 * b:256 * b + 128], xeven[:, 128 * m:128 * m + 128], ident[:])
+                nc.tensor.transpose(tpx[:, 256 * b + 128:256 * b + 256], xf[:, 256 * m + 128:256 * m + 256], ident[:])
             nc.scalar.copy(out=xgf[:, 512 * g:512 * g + 512].rearrange("q (b s u) -> q b s u", b=2, u=2),
                            in_=tpx[:].rearrange("q (b u s) -> q b s u", b=2, u=2))
 
@@ -97,40 +105,32 @@ def tile_attention_pa_kernel(tc, hidden_states, cos, sin, w_qkv, out_0, out_1, o
         nc.gpsimd.tensor_scalar(out=sind_v[:, :, 0], in0=sin_v[:, :, 0], scalar1=-1.0, scalar2=None, op0=MULT)
         nc.gpsimd.tensor_copy(out=sind_v[:, :, 1], in_=sin_v[:, :, 1])
 
-        splits = {}
+        evens = {}
         grps = {}
         codes = {}
         accs = {}
         osts = {}
 
-        def split_part(u, engine_copy, c0, c1):
-            src = wraws[u][:].bitcast(F32).rearrange("p (c u w) -> p u c w", u=2, w=8)
-            dst = splits[u][:].rearrange("p (u c w) -> p u c w", u=2, w=8)
-            engine_copy(out=dst[:, :, c0:c1, :], in_=src[:, :, c0:c1, :])
-
-        def split_words(u):
-            split = spool.tile([P, 2048], F32, tag="split")
-            splits[u] = split
-            if u == 0:
-                for hf in range(2):
-                    for j in range(2):
-                        c0 = 64 * j + 32 * hf
-                        split_part(u, nc.vector.tensor_copy, c0, c0 + 32)
-            else:
-                split_part(u, nc.vector.tensor_copy, 0, 128 - SCALAR_CHUNKS)
-                split_part(u, nc.scalar.copy, 128 - SCALAR_CHUNKS, 128)
+        def split(u, copy):
+            wf = wraws[u][:].bitcast(F32)
+            even = epool.tile([P, 1024], F32, tag="even")
+            evens[u] = even
+            parts = ((0, 2), (4, 6), (2, 4), (6, 8)) if u == 0 else ((0, 8),)
+            for m0, m1 in parts:
+                gather_even(wf, even, m0, m1)
+                move_odd(wf, copy, m0, m1)
 
         def transposes(u):
+            wf = wraws[u][:].bitcast(F32)
             grp = gpool.tile([P, 4096], BF16, align_bytes=64, tag="grp")
             grps[u] = grp
             gf = grp[:].bitcast(F32)
             for g in range(4):
                 tp = psum_t.tile([P, 512], F32, tag="tp")
                 for j in range(2):
-                    for h in range(2):
-                        i = 1024 * h + 512 * j + 128 * g
-                        o = 256 * j + 128 * h
-                        nc.tensor.transpose(tp[:, o:o + 128], splits[u][:, i:i + 128], ident[:])
+                    m = 4 * j + g
+                    nc.tensor.transpose(tp[:, 256 * j:256 * j + 128], evens[u][:, 128 * m:128 * m + 128], ident[:])
+                    nc.tensor.transpose(tp[:, 256 * j + 128:256 * j + 256], wf[:, 256 * m + 128:256 * m + 256], ident[:])
                 nc.scalar.copy(out=gf[:, 512 * g:512 * g + 512].rearrange("q (j c u) -> q j c u", j=2, u=2),
                                in_=tp[:].rearrange("q (j u c) -> q j c u", j=2, u=2))
 
@@ -177,10 +177,21 @@ def tile_attention_pa_kernel(tc, hidden_states, cos, sin, w_qkv, out_0, out_1, o
                     in0=acc[:].rearrange("p (h i e) -> p h i e", h=4, e=2)[:, :, :, ::-1],
                     in1=sind[:].rearrange("p (i e) -> p i e", e=2).unsqueeze(1).to_broadcast([P, 4, 64, 2]),
                     op=MULT)
-                nc.gpsimd.tensor_tensor(out=dst, in0=t1[:].rearrange("p (b m) -> p b m", b=2),
-                                        in1=t2[:].rearrange("p (b m) -> p b m", b=2), op=ADD)
-            else:
-                nc.scalar.copy(out=dst, in_=acc[:].rearrange("p (b m) -> p b m", b=2))
+
+                def add():
+                    nc.vector.tensor_tensor(out=dst, in0=t1[:].rearrange("p (b m) -> p b m", b=2),
+                                            in1=t2[:].rearrange("p (b m) -> p b m", b=2), op=ADD)
+                    store(u, dst)
+
+                return add
+            nc.scalar.copy(out=dst, in_=acc[:].rearrange("p (b m) -> p b m", b=2))
+            store(u, dst)
+            return None
+
+        def store(u, dst):
+            kind, hc = groups[u // 2]
+            jp = u % 2
+            ost = osts[u // 2]
             o_dram = outs[kind].rearrange("b s h l -> s b (h l)")
             if u // 2 == NUNIT // 2 - 1:
                 lo = 512 * hc + 256 * jp
@@ -189,19 +200,22 @@ def tile_attention_pa_kernel(tc, hidden_states, cos, sin, w_qkv, out_0, out_1, o
                 nc.sync.dma_start(out=o_dram[:, :, 512 * hc:512 * hc + 512],
                                   in_=ost[:].rearrange("p (b m) -> p b m", b=2))
 
-        split_words(0)
+        split(0, nc.scalar.copy)
         for hf in range(2):
             nc.vector.quantize_mx(out=xc[:, 512 * hf:512 * hf + 512].bitcast(FP8X4),
                                   scales=xs[:, 512 * hf:512 * hf + 512],
                                   in_=xgrp[:, 2048 * hf:2048 * hf + 2048])
+        split(1, nc.scalar.copy)
         for u in range(NUNIT + 3):
-            if u + 1 < NUNIT:
-                split_words(u + 1)
             if u < NUNIT:
                 transposes(u)
             if 2 <= u < NUNIT + 2:
                 matmuls(u - 2)
-            if u >= 3:
-                finish(u - 3)
+            if u + 2 < NUNIT:
+                plain_step = u >= 3 and PATTERN[(u - 3) // 2] == "V"
+                split(u + 2, nc.vector.tensor_copy if plain_step else nc.scalar.copy)
+            add = finish(u - 3) if u >= 3 else None
             if 1 <= u < NUNIT + 1:
                 quantise(u - 1)
+            if add:
+                add()

@@ -22,6 +22,7 @@ GRP_BUFS = 3
 CODE_BUFS = 3
 ROT_BUFS = 3
 OUT_BUFS = 8
+NS = 3
 
 
 def tile_attention_pa_kernel(tc, hidden_states, cos, sin, w_qkv, out_0, out_1, out_2):
@@ -46,11 +47,20 @@ def tile_attention_pa_kernel(tc, hidden_states, cos, sin, w_qkv, out_0, out_1, o
 
         ident = const.tile([P, P], F32)
         make_identity(nc, ident[:])
+        def load(raw, src, k0, k1):
+            edge = 512 * NS
+            for lo, hi, base in ((0, edge, 0), (edge, 2048, 2 * edge)):
+                a, z = max(lo, k0), min(hi, k1)
+                if a < z:
+                    sb = raw[:, base:base + 2 * (hi - lo)].rearrange("p (j k) -> p j k", j=2)
+                    nc.sync.dma_start(out=sb[:, :, a - lo:z - lo], in_=src[:, :, a:z])
+
         xraw = const.tile([P, 4096], BF16)
         x_dram = hidden_states.rearrange("b s k -> s b k")
-        x_sb = xraw[:].rearrange("p (b k) -> p b k", b=2)
-        for k0 in range(0, 2048, 1024):
-            nc.sync.dma_start(out=x_sb[:, :, k0:k0 + 1024], in_=x_dram[:, :, k0:k0 + 1024])
+        load(xraw, x_dram, 0, 1024)
+        load(xraw, x_dram, 1024, 2048)
+        warm = const.tile([P, 1], F32)
+        nc.scalar.copy(out=warm[:], in_=ident[:, 0:1])
         cos_raw = const.tile([P, P], BF16)
         sin_raw = const.tile([P, P], BF16)
         nc.scalar.dma_start(out=cos_raw[:], in_=cos)
@@ -62,11 +72,10 @@ def tile_attention_pa_kernel(tc, hidden_states, cos, sin, w_qkv, out_0, out_1, o
             r0 = 2048 * kind + 512 * hc + 256 * (u % 2)
             wraw = wpool.tile([P, 4096], BF16)
             wraws.append(wraw)
-            w_sb = wraw[:].rearrange("p (j k) -> p j k", j=2)
             w_dram = w_qkv[r0:r0 + 256, :].rearrange("(j p) k -> p j k", j=2)
             step = 1024 if u == 0 else 2048
             for k0 in range(0, 2048, step):
-                nc.sync.dma_start(out=w_sb[:, :, k0:k0 + step], in_=w_dram[:, :, k0:k0 + step])
+                load(wraw, w_dram, k0, k0 + step)
 
         def gather_even(words, even, m0, m1):
             nc.vector.tensor_copy(
@@ -78,22 +87,30 @@ def tile_attention_pa_kernel(tc, hidden_states, cos, sin, w_qkv, out_0, out_1, o
             copy(out=view[:, 1, 0], in_=view[:, 0, 1])
 
         xf = xraw[:].bitcast(F32)
-        xeven = const.tile([P, 1024], F32)
+        xeven = const.tile([P, 256 * NS], F32)
         xgrp = const.tile([P, 4096], BF16, align_bytes=64)
         xgf = xgrp[:].bitcast(F32)
         xc = const.tile([P, 1024], U32, align_bytes=64)
         xs = const.tile([P, 1024], U8, align_bytes=64)
-        for hf in range(2):
+        def transpose_pair(dst, words, even, j, g):
+            if g < NS:
+                m = NS * j + g
+                slots = (even[:, 128 * m:128 * m + 128], words[:, 256 * m + 128:256 * m + 256])
+            else:
+                o = 512 * NS + 256 * ((4 - NS) * j + g - NS)
+                slots = (words[:, o:o + 256:2], words[:, o + 1:o + 256:2])
+            for h in range(2):
+                nc.tensor.transpose(dst[:, 256 * j + 128 * h:256 * j + 128 * h + 128], slots[h], ident[:])
+
+        for g in range(NS):
             for b in range(2):
-                m = 4 * b + 2 * hf
-                gather_even(xf, xeven, m, m + 2)
-                move_odd(xf, nc.scalar.copy, m, m + 2)
+                m = NS * b + g
+                gather_even(xf, xeven, m, m + 1)
+                move_odd(xf, nc.scalar.copy, m, m + 1)
         for g in range(4):
             tpx = psum_t.tile([P, 512], F32, tag="tp")
             for b in range(2):
-                m = 4 * b + g
-                nc.tensor.transpose(tpx[:, 256 * b:256 * b + 128], xeven[:, 128 * m:128 * m + 128], ident[:])
-                nc.tensor.transpose(tpx[:, 256 * b + 128:256 * b + 256], xf[:, 256 * m + 128:256 * m + 256], ident[:])
+                transpose_pair(tpx, xf, xeven, b, g)
             nc.scalar.copy(out=xgf[:, 512 * g:512 * g + 512].rearrange("q (b s u) -> q b s u", b=2, u=2),
                            in_=tpx[:].rearrange("q (b u s) -> q b s u", b=2, u=2))
 
@@ -113,9 +130,9 @@ def tile_attention_pa_kernel(tc, hidden_states, cos, sin, w_qkv, out_0, out_1, o
 
         def split(u, copy):
             wf = wraws[u][:].bitcast(F32)
-            even = epool.tile([P, 1024], F32, tag="even")
+            even = epool.tile([P, 256 * NS], F32, tag="even")
             evens[u] = even
-            parts = ((0, 2), (4, 6), (2, 4), (6, 8)) if u == 0 else ((0, 8),)
+            parts = [(NS * j + g, NS * j + g + 1) for g in range(NS) for j in range(2)] if u == 0 else [(0, 2 * NS)]
             for m0, m1 in parts:
                 gather_even(wf, even, m0, m1)
                 move_odd(wf, copy, m0, m1)
@@ -128,9 +145,7 @@ def tile_attention_pa_kernel(tc, hidden_states, cos, sin, w_qkv, out_0, out_1, o
             for g in range(4):
                 tp = psum_t.tile([P, 512], F32, tag="tp")
                 for j in range(2):
-                    m = 4 * j + g
-                    nc.tensor.transpose(tp[:, 256 * j:256 * j + 128], evens[u][:, 128 * m:128 * m + 128], ident[:])
-                    nc.tensor.transpose(tp[:, 256 * j + 128:256 * j + 256], wf[:, 256 * m + 128:256 * m + 256], ident[:])
+                    transpose_pair(tp, wf, evens[u], j, g)
                 nc.scalar.copy(out=gf[:, 512 * g:512 * g + 512].rearrange("q (j c u) -> q j c u", j=2, u=2),
                                in_=tp[:].rearrange("q (j u c) -> q j c u", j=2, u=2))
 

@@ -55,16 +55,16 @@ def tile_attention_pa_kernel(tc, hidden_states, cos, sin, w_qkv, out_0, out_1, o
                     sb = raw[:, base:base + 2 * (hi - lo)].rearrange("p (j k) -> p j k", j=2)
                     nc.sync.dma_start(out=sb[:, :, a - lo:z - lo], in_=src[:, :, a:z])
 
-        xraw = const.tile([P, 4096], BF16)
-        x_dram = hidden_states.rearrange("b s k -> s b k")
-        load(xraw, x_dram, 0, 1024)
-        load(xraw, x_dram, 1024, 2048)
-        warm = const.tile([P, 1], F32)
-        nc.scalar.copy(out=warm[:], in_=ident[:, 0:1])
         cos_raw = const.tile([P, P], BF16)
         sin_raw = const.tile([P, P], BF16)
         nc.scalar.dma_start(out=cos_raw[:], in_=cos)
         nc.scalar.dma_start(out=sin_raw[:], in_=sin)
+        warm = const.tile([P, 1], F32)
+        nc.scalar.copy(out=warm[:], in_=ident[:, 0:1])
+        xraw = const.tile([P, 4096], BF16)
+        x_dram = hidden_states.rearrange("b s k -> s b k")
+        load(xraw, x_dram, 0, 1024)
+        load(xraw, x_dram, 1024, 2048)
 
         wraws = []
         for u in range(NUNIT):
@@ -128,14 +128,16 @@ def tile_attention_pa_kernel(tc, hidden_states, cos, sin, w_qkv, out_0, out_1, o
         accs = {}
         osts = {}
 
-        def split(u, copy):
+        def gather_unit(u):
             wf = wraws[u][:].bitcast(F32)
             even = epool.tile([P, 256 * NS], F32, tag="even")
             evens[u] = even
             parts = [(NS * j + g, NS * j + g + 1) for g in range(NS) for j in range(2)] if u == 0 else [(0, 2 * NS)]
             for m0, m1 in parts:
                 gather_even(wf, even, m0, m1)
-                move_odd(wf, copy, m0, m1)
+
+        def move_unit(u, copy):
+            move_odd(wraws[u][:].bitcast(F32), copy, 0, 2 * NS)
 
         def transposes(u):
             wf = wraws[u][:].bitcast(F32)
@@ -194,7 +196,7 @@ def tile_attention_pa_kernel(tc, hidden_states, cos, sin, w_qkv, out_0, out_1, o
                     op=MULT)
 
                 def add():
-                    nc.vector.tensor_tensor(out=dst, in0=t1[:].rearrange("p (b m) -> p b m", b=2),
+                    nc.gpsimd.tensor_tensor(out=dst, in0=t1[:].rearrange("p (b m) -> p b m", b=2),
                                             in1=t2[:].rearrange("p (b m) -> p b m", b=2), op=ADD)
                     store(u, dst)
 
@@ -215,22 +217,29 @@ def tile_attention_pa_kernel(tc, hidden_states, cos, sin, w_qkv, out_0, out_1, o
                 nc.sync.dma_start(out=o_dram[:, :, 512 * hc:512 * hc + 512],
                                   in_=ost[:].rearrange("p (b m) -> p b m", b=2))
 
-        split(0, nc.scalar.copy)
+        gather_unit(0)
+        move_unit(0, nc.vector.tensor_copy)
         for hf in range(2):
             nc.vector.quantize_mx(out=xc[:, 512 * hf:512 * hf + 512].bitcast(FP8X4),
                                   scales=xs[:, 512 * hf:512 * hf + 512],
                                   in_=xgrp[:, 2048 * hf:2048 * hf + 2048])
-        split(1, nc.scalar.copy)
+        gather_unit(1)
+        move_unit(1, nc.vector.tensor_copy)
         for u in range(NUNIT + 3):
             if u < NUNIT:
                 transposes(u)
             if 2 <= u < NUNIT + 2:
                 matmuls(u - 2)
             if u + 2 < NUNIT:
-                plain_step = u >= 3 and PATTERN[(u - 3) // 2] == "V"
-                split(u + 2, nc.vector.tensor_copy if plain_step else nc.scalar.copy)
+                gather_unit(u + 2)
+            rotated_step = u >= 3 and PATTERN[(u - 3) // 2] == "R"
+            if not rotated_step and 1 <= u < NUNIT + 1:
+                quantise(u - 1)
             add = finish(u - 3) if u >= 3 else None
-            if 1 <= u < NUNIT + 1:
+            if u + 2 < NUNIT:
+                on_scalar = rotated_step and u % 2 == 0
+                move_unit(u + 2, nc.scalar.copy if on_scalar else nc.vector.tensor_copy)
+            if rotated_step and 1 <= u < NUNIT + 1:
                 quantise(u - 1)
             if add:
                 add()

@@ -48,12 +48,8 @@ def tile_attention_pa_kernel(tc, hidden_states, cos, sin, w_qkv, out_0, out_1, o
         ident = const.tile([P, P], F32)
         make_identity(nc, ident[:])
         def load(raw, src, k0, k1):
-            edge = 512 * NS
-            for lo, hi, base in ((0, edge, 0), (edge, 2048, 2 * edge)):
-                a, z = max(lo, k0), min(hi, k1)
-                if a < z:
-                    sb = raw[:, base:base + 2 * (hi - lo)].rearrange("p (j k) -> p j k", j=2)
-                    nc.sync.dma_start(out=sb[:, :, a - lo:z - lo], in_=src[:, :, a:z])
+            sb = raw[:].rearrange("p (j k) -> p j k", j=2)
+            nc.sync.dma_start(out=sb[:, :, k0:k1], in_=src[:, :, k0:k1])
 
         cos_raw = const.tile([P, P], BF16)
         sin_raw = const.tile([P, P], BF16)
@@ -63,7 +59,8 @@ def tile_attention_pa_kernel(tc, hidden_states, cos, sin, w_qkv, out_0, out_1, o
         nc.scalar.copy(out=warm[:], in_=ident[:, 0:1])
         xraw = const.tile([P, 4096], BF16)
         x_dram = hidden_states.rearrange("b s k -> s b k")
-        load(xraw, x_dram, 0, 1024)
+        load(xraw, x_dram, 0, 512)
+        load(xraw, x_dram, 512, 1024)
         load(xraw, x_dram, 1024, 2048)
 
         wraws = []
@@ -77,14 +74,16 @@ def tile_attention_pa_kernel(tc, hidden_states, cos, sin, w_qkv, out_0, out_1, o
             for k0 in range(0, 2048, step):
                 load(wraw, w_dram, k0, k0 + step)
 
-        def gather_even(words, even, m0, m1):
-            nc.vector.tensor_copy(
-                out=even[:, 128 * m0:128 * m1].rearrange("p (m c s w) -> p m c s w", c=8, s=2, w=8),
-                in_=words[:, 256 * m0:256 * m1].rearrange("p (m s c v w) -> p v m c s w", s=2, c=8, v=2, w=8)[:, 0])
+        def gather_even(words, even, rows=slice(0, 2), passes=slice(0, NS)):
+            src = words.rearrange("p (j g s c v w) -> p v j g s c w", j=2, g=4, s=2, v=2, w=8)
+            dst = even.rearrange("p (j g c s w) -> p j g s c w", j=2, g=NS, s=2, w=8)
+            nc.vector.tensor_copy(out=dst[:, rows, passes], in_=src[:, 0, rows, passes])
 
-        def move_odd(words, copy, m0, m1):
-            view = words[:, 256 * m0:256 * m1].rearrange("p (m s c v w) -> p s v m c w", s=2, c=8, v=2, w=8)
-            copy(out=view[:, 1, 0], in_=view[:, 0, 1])
+        def move_odd(words, copy, rows=slice(0, 2), passes=slice(0, NS)):
+            view = words.rearrange("p (j g s c v w) -> p v s j g c w", j=2, g=4, s=2, v=2, w=8)
+            copy(out=view[:, 0, 1, rows, passes], in_=view[:, 1, 0, rows, passes])
+
+        pieces = [(slice(j, j + 1), slice(g, g + 1)) for g in range(NS) for j in range(2)]
 
         xf = xraw[:].bitcast(F32)
         xeven = const.tile([P, 256 * NS], F32)
@@ -95,24 +94,23 @@ def tile_attention_pa_kernel(tc, hidden_states, cos, sin, w_qkv, out_0, out_1, o
         def transpose_pair(dst, words, even, j, g):
             if g < NS:
                 m = NS * j + g
-                slots = (even[:, 128 * m:128 * m + 128], words[:, 256 * m + 128:256 * m + 256])
+                o = 1024 * j + 256 * g
+                slots = (even[:, 128 * m:128 * m + 128], words[:, o + 128:o + 256])
             else:
-                o = 512 * NS + 256 * ((4 - NS) * j + g - NS)
+                o = 1024 * j + 256 * g
                 slots = (words[:, o:o + 256:2], words[:, o + 1:o + 256:2])
             for h in range(2):
                 nc.tensor.transpose(dst[:, 256 * j + 128 * h:256 * j + 128 * h + 128], slots[h], ident[:])
 
-        for g in range(NS):
-            for b in range(2):
-                m = NS * b + g
-                gather_even(xf, xeven, m, m + 1)
-                move_odd(xf, nc.scalar.copy, m, m + 1)
+        for rows, passes in pieces:
+            gather_even(xf, xeven[:], rows, passes)
+            move_odd(xf, nc.scalar.copy, rows, passes)
         for g in range(4):
             tpx = psum_t.tile([P, 512], F32, tag="tp")
             for b in range(2):
                 transpose_pair(tpx, xf, xeven, b, g)
             nc.scalar.copy(out=xgf[:, 512 * g:512 * g + 512].rearrange("q (b s u) -> q b s u", b=2, u=2),
-                           in_=tpx[:].rearrange("q (b u s) -> q b s u", b=2, u=2))
+                     in_=tpx[:].rearrange("q (b u s) -> q b s u", b=2, u=2))
 
         cosd = const.tile([P, P], F32)
         sind = const.tile([P, P], F32)
@@ -126,18 +124,21 @@ def tile_attention_pa_kernel(tc, hidden_states, cos, sin, w_qkv, out_0, out_1, o
         grps = {}
         codes = {}
         accs = {}
+        bank = {}
         osts = {}
 
         def gather_unit(u):
             wf = wraws[u][:].bitcast(F32)
             even = epool.tile([P, 256 * NS], F32, tag="even")
             evens[u] = even
-            parts = [(NS * j + g, NS * j + g + 1) for g in range(NS) for j in range(2)] if u == 0 else [(0, 2 * NS)]
-            for m0, m1 in parts:
-                gather_even(wf, even, m0, m1)
+            if u == 0:
+                for rows, passes in pieces:
+                    gather_even(wf, even[:], rows, passes)
+            else:
+                gather_even(wf, even[:])
 
         def move_unit(u, copy):
-            move_odd(wraws[u][:].bitcast(F32), copy, 0, 2 * NS)
+            move_odd(wraws[u][:].bitcast(F32), copy)
 
         def transposes(u):
             wf = wraws[u][:].bitcast(F32)
@@ -162,22 +163,29 @@ def tile_attention_pa_kernel(tc, hidden_states, cos, sin, w_qkv, out_0, out_1, o
                                       in_=grps[u][:, 4 * n * i:4 * n * i + 4 * n])
 
         def matmuls(u):
-            acc = psum_a.tile([P, 512], F32, tag="acc")
-            accs[u] = acc
             wc, ws = codes[u]
-            for b in range(2):
-                for g in range(4):
-                    xo = 256 * g + 128 * b
-                    nc.tensor.matmul_mx(out=acc[:, 256 * b:256 * b + 256],
-                                        lhsT=xc[:, xo:xo + 128].bitcast(FP8X4), lhsT_scale=xs[:, xo:xo + 128],
-                                        rhs=wc[:, 256 * g:256 * g + 256].bitcast(FP8X4),
-                                        rhs_scale=ws[:, 256 * g:256 * g + 256],
-                                        start=(g == 0), stop=(g == 3))
+            if u == NUNIT - 1:
+                acc_b = [psum_a.tile([P, 512], F32, tag="acc", name="acc_b%d" % b) for b in range(2)]
+                accs[u] = [acc_b[b][:, 0:256] for b in range(2)]
+                order = [(b, g) for g in range(4) for b in range(2)]
+            else:
+                acc = psum_a.tile([P, 512], F32, tag="acc")
+                accs[u] = [acc[:, 256 * b:256 * b + 256] for b in range(2)]
+                order = [(b, g) for b in range(2) for g in range(4)]
+                bank[u] = acc
+            for b, g in order:
+                xo = 256 * g + 128 * b
+                nc.tensor.matmul_mx(out=accs[u][b],
+                                    lhsT=xc[:, xo:xo + 128].bitcast(FP8X4), lhsT_scale=xs[:, xo:xo + 128],
+                                    rhs=wc[:, 256 * g:256 * g + 256].bitcast(FP8X4),
+                                    rhs_scale=ws[:, 256 * g:256 * g + 256],
+                                    start=(g == 0), stop=(g == 3))
 
         def finish(u):
             kind, hc = groups[u // 2]
             jp = u % 2
-            acc = accs[u]
+            if u < NUNIT - 1:
+                acc = bank[u]
             if jp == 0:
                 ost = opool.tile([P, 1024], F32, tag="ost")
                 osts[u // 2] = ost
@@ -201,6 +209,13 @@ def tile_attention_pa_kernel(tc, hidden_states, cos, sin, w_qkv, out_0, out_1, o
                     store(u, dst)
 
                 return add
+            if u == NUNIT - 1:
+                nc.vector.tensor_copy(out=dst[:, 0, :], in_=accs[u][0])
+                nc.scalar.copy(out=dst[:, 1, :], in_=accs[u][1])
+                for b in range(2):
+                    nc.sync.dma_start(out=outs[kind].rearrange("b s h l -> s b (h l)")[:, b, 512 * hc + 256:512 * hc + 512],
+                                      in_=dst[:, b, :])
+                return None
             nc.scalar.copy(out=dst, in_=acc[:].rearrange("p (b m) -> p b m", b=2))
             store(u, dst)
             return None
@@ -230,16 +245,14 @@ def tile_attention_pa_kernel(tc, hidden_states, cos, sin, w_qkv, out_0, out_1, o
                 transposes(u)
             if 2 <= u < NUNIT + 2:
                 matmuls(u - 2)
-            if u + 2 < NUNIT:
-                gather_unit(u + 2)
             rotated_step = u >= 3 and PATTERN[(u - 3) // 2] == "R"
-            if not rotated_step and 1 <= u < NUNIT + 1:
-                quantise(u - 1)
             add = finish(u - 3) if u >= 3 else None
             if u + 2 < NUNIT:
-                on_scalar = rotated_step and u % 2 == 0
-                move_unit(u + 2, nc.scalar.copy if on_scalar else nc.vector.tensor_copy)
-            if rotated_step and 1 <= u < NUNIT + 1:
+                gather_unit(u + 2)
+            if 1 <= u < NUNIT + 1:
                 quantise(u - 1)
+            if u + 2 < NUNIT:
+                on_scalar = u < 3 or (rotated_step and u % 2 == 0)
+                move_unit(u + 2, nc.scalar.copy if on_scalar else nc.vector.tensor_copy)
             if add:
                 add()

from contextlib import ExitStack

import concourse.mybir as mybir
from concourse.masks import make_identity

F32 = mybir.dt.float32
BF16 = mybir.dt.bfloat16
U32 = mybir.dt.uint32
U8 = mybir.dt.uint8
FP8X4 = mybir.dt.float8_e4m3fn_x4
MULT = mybir.AluOpType.mult
ADD = mybir.AluOpType.add

FLOPS = 2 * 256 * 6144 * 2048

P = 128
NUNIT = 24
PATTERN = "RRVRRVRRVRRV"
W_BUFS = 11
EVEN_BUFS = 4
GRP_BUFS = 3
CODE_BUFS = 3
ROT_BUFS = 3
OUT_BUFS = 8
NS = 3


def tile_attention_pa_kernel(tc, hidden_states, cos, sin, w_qkv, out_0, out_1, out_2):
    nc = tc.nc
    outs = (out_0, out_1, out_2)
    rotated = [(kind, hc) for hc in range(4) for kind in range(2)]
    plain = [(2, hc) for hc in range(4)]
    groups = []
    for ch in PATTERN:
        groups.append(rotated.pop(0) if ch == "R" else plain.pop(0))
    with ExitStack() as ctx:
        const = ctx.enter_context(tc.tile_pool(name="const", bufs=1))
        wpool = ctx.enter_context(tc.tile_pool(name="wpool", bufs=W_BUFS))
        epool = ctx.enter_context(tc.tile_pool(name="epool", bufs=EVEN_BUFS))
        gpool = ctx.enter_context(tc.tile_pool(name="gpool", bufs=GRP_BUFS))
        cpool = ctx.enter_context(tc.tile_pool(name="cpool", bufs=CODE_BUFS))
        rpool = ctx.enter_context(tc.tile_pool(name="rpool", bufs=ROT_BUFS))
        opool = ctx.enter_context(tc.tile_pool(name="opool", bufs=OUT_BUFS))
        psum_t = ctx.enter_context(tc.psum_pool(name="psum_t", bufs=4))
        psum_a = ctx.enter_context(tc.psum_pool(name="psum_a", bufs=4))
        ctx.enter_context(tc.manual_schedule())

        ident = const.tile([P, P], F32)
        make_identity(nc, ident[:])
        def load(raw, src, k0, k1):
            sb = raw[:].rearrange("p (j k) -> p j k", j=2)
            nc.sync.dma_start(out=sb[:, :, k0:k1], in_=src[:, :, k0:k1])

        cos_raw = const.tile([P, P], BF16)
        sin_raw = const.tile([P, P], BF16)
        nc.scalar.dma_start(out=cos_raw[:], in_=cos)
        nc.scalar.dma_start(out=sin_raw[:], in_=sin)
        warm = const.tile([P, 1], F32)
        nc.scalar.copy(out=warm[:], in_=ident[:, 0:1])
        xraw = const.tile([P, 4096], BF16)
        x_dram = hidden_states.rearrange("b s k -> s b k")
        load(xraw, x_dram, 0, 512)
        load(xraw, x_dram, 512, 1024)
        load(xraw, x_dram, 1024, 2048)

        wraws = []
        for u in range(NUNIT):
            kind, hc = groups[u // 2]
            r0 = 2048 * kind + 512 * hc + 256 * (u % 2)
            wraw = wpool.tile([P, 4096], BF16)
            wraws.append(wraw)
            w_dram = w_qkv[r0:r0 + 256, :].rearrange("(j p) k -> p j k", j=2)
            step = 1024 if u == 0 else 2048
            for k0 in range(0, 2048, step):
                load(wraw, w_dram, k0, k0 + step)

        def gather_even(words, even, rows=slice(0, 2), passes=slice(0, NS)):
            src = words.rearrange("p (j g s c v w) -> p v j g s c w", j=2, g=4, s=2, v=2, w=8)
            dst = even.rearrange("p (j g c s w) -> p j g s c w", j=2, g=NS, s=2, w=8)
            nc.vector.tensor_copy(out=dst[:, rows, passes], in_=src[:, 0, rows, passes])

        def move_odd(words, copy, rows=slice(0, 2), passes=slice(0, NS)):
            view = words.rearrange("p (j g s c v w) -> p v s j g c w", j=2, g=4, s=2, v=2, w=8)
            copy(out=view[:, 0, 1, rows, passes], in_=view[:, 1, 0, rows, passes])

        pieces = [(slice(j, j + 1), slice(g, g + 1)) for g in range(NS) for j in range(2)]

        xf = xraw[:].bitcast(F32)
        xeven = const.tile([P, 256 * NS], F32)
        xgrp = const.tile([P, 4096], BF16, align_bytes=64)
        xgf = xgrp[:].bitcast(F32)
        xc = const.tile([P, 1024], U32, align_bytes=64)
        xs = const.tile([P, 1024], U8, align_bytes=64)
        def transpose_pair(dst, words, even, j, g):
            if g < NS:
                m = NS * j + g
                o = 1024 * j + 256 * g
                slots = (even[:, 128 * m:128 * m + 128], words[:, o + 128:o + 256])
            else:
                o = 1024 * j + 256 * g
                slots = (words[:, o:o + 256:2], words[:, o + 1:o + 256:2])
            for h in range(2):
                nc.tensor.transpose(dst[:, 256 * j + 128 * h:256 * j + 128 * h + 128], slots[h], ident[:])

        for rows, passes in pieces:
            gather_even(xf, xeven[:], rows, passes)
            move_odd(xf, nc.scalar.copy, rows, passes)
        for g in range(4):
            tpx = psum_t.tile([P, 512], F32, tag="tp")
            for b in range(2):
                transpose_pair(tpx, xf, xeven, b, g)
            nc.scalar.copy(out=xgf[:, 512 * g:512 * g + 512].rearrange("q (b s u) -> q b s u", b=2, u=2),
                     in_=tpx[:].rearrange("q (b u s) -> q b s u", b=2, u=2))

        cosd = const.tile([P, P], F32)
        sind = const.tile([P, P], F32)
        nc.gpsimd.tensor_copy(out=cosd[:], in_=cos_raw[:])
        sin_v = sin_raw[:].rearrange("p (i e) -> p i e", e=2)
        sind_v = sind[:].rearrange("p (i e) -> p i e", e=2)
        nc.gpsimd.tensor_scalar(out=sind_v[:, :, 0], in0=sin_v[:, :, 0], scalar1=-1.0, scalar2=None, op0=MULT)
        nc.gpsimd.tensor_copy(out=sind_v[:, :, 1], in_=sin_v[:, :, 1])

        evens = {}
        grps = {}
        codes = {}
        accs = {}
        bank = {}
        osts = {}

        def gather_unit(u):
            wf = wraws[u][:].bitcast(F32)
            even = epool.tile([P, 256 * NS], F32, tag="even")
            evens[u] = even
            if u == 0:
                for rows, passes in pieces:
                    gather_even(wf, even[:], rows, passes)
            else:
                gather_even(wf, even[:])

        def move_unit(u, copy):
            move_odd(wraws[u][:].bitcast(F32), copy)

        def transposes(u):
            wf = wraws[u][:].bitcast(F32)
            grp = gpool.tile([P, 4096], BF16, align_bytes=64, tag="grp")
            grps[u] = grp
            gf = grp[:].bitcast(F32)
            for g in range(4):
                tp = psum_t.tile([P, 512], F32, tag="tp")
                for j in range(2):
                    transpose_pair(tp, wf, evens[u], j, g)
                nc.scalar.copy(out=gf[:, 512 * g:512 * g + 512].rearrange("q (j c u) -> q j c u", j=2, u=2),
                               in_=tp[:].rearrange("q (j u c) -> q j c u", j=2, u=2))

        def quantise(u):
            wc = cpool.tile([P, 1024], U32, align_bytes=64, tag="wc")
            ws = cpool.tile([P, 1024], U8, align_bytes=64, tag="ws")
            codes[u] = (wc, ws)
            pieces = 4 if u == NUNIT - 1 else 1
            n = 1024 // pieces
            for i in range(pieces):
                nc.vector.quantize_mx(out=wc[:, n * i:n * i + n].bitcast(FP8X4), scales=ws[:, n * i:n * i + n],
                                      in_=grps[u][:, 4 * n * i:4 * n * i + 4 * n])

        def matmuls(u):
            wc, ws = codes[u]
            if u == NUNIT - 1:
                acc_b = [psum_a.tile([P, 512], F32, tag="acc", name="acc_b%d" % b) for b in range(2)]
                accs[u] = [acc_b[b][:, 0:256] for b in range(2)]
                order = [(b, g) for g in range(4) for b in range(2)]
            else:
                acc = psum_a.tile([P, 512], F32, tag="acc")
                accs[u] = [acc[:, 256 * b:256 * b + 256] for b in range(2)]
                order = [(b, g) for b in range(2) for g in range(4)]
                bank[u] = acc
            for b, g in order:
                xo = 256 * g + 128 * b
                nc.tensor.matmul_mx(out=accs[u][b],
                                    lhsT=xc[:, xo:xo + 128].bitcast(FP8X4), lhsT_scale=xs[:, xo:xo + 128],
                                    rhs=wc[:, 256 * g:256 * g + 256].bitcast(FP8X4),
                                    rhs_scale=ws[:, 256 * g:256 * g + 256],
                                    start=(g == 0), stop=(g == 3))

        def finish(u):
            kind, hc = groups[u // 2]
            jp = u % 2
            if u < NUNIT - 1:
                acc = bank[u]
            if jp == 0:
                ost = opool.tile([P, 1024], F32, tag="ost")
                osts[u // 2] = ost
            ost = osts[u // 2]
            dst = ost[:].rearrange("p (b m) -> p b m", b=2)[:, :, 256 * jp:256 * jp + 256]
            if kind < 2:
                t1 = rpool.tile([P, 512], F32, tag="t1")
                t2 = rpool.tile([P, 512], F32, tag="t2")
                nc.vector.tensor_tensor(out=t1[:].rearrange("p (h m) -> p h m", h=4),
                                        in0=acc[:].rearrange("p (h m) -> p h m", h=4),
                                        in1=cosd[:].unsqueeze(1).to_broadcast([P, 4, P]), op=MULT)
                nc.vector.tensor_tensor(
                    out=t2[:].rearrange("p (h i e) -> p h i e", h=4, e=2),
                    in0=acc[:].rearrange("p (h i e) -> p h i e", h=4, e=2)[:, :, :, ::-1],
                    in1=sind[:].rearrange("p (i e) -> p i e", e=2).unsqueeze(1).to_broadcast([P, 4, 64, 2]),
                    op=MULT)

                def add():
                    nc.gpsimd.tensor_tensor(out=dst, in0=t1[:].rearrange("p (b m) -> p b m", b=2),
                                            in1=t2[:].rearrange("p (b m) -> p b m", b=2), op=ADD)
                    store(u, dst)

                return add
            if u == NUNIT - 1:
                nc.vector.tensor_copy(out=dst[:, 0, :], in_=accs[u][0])
                nc.scalar.copy(out=dst[:, 1, :], in_=accs[u][1])
                for b in range(2):
                    nc.sync.dma_start(out=outs[kind].rearrange("b s h l -> s b (h l)")[:, b, 512 * hc + 256:512 * hc + 512],
                                      in_=dst[:, b, :])
                return None
            nc.scalar.copy(out=dst, in_=acc[:].rearrange("p (b m) -> p b m", b=2))
            store(u, dst)
            return None

        def store(u, dst):
            kind, hc = groups[u // 2]
            jp = u % 2
            ost = osts[u // 2]
            o_dram = outs[kind].rearrange("b s h l -> s b (h l)")
            if u // 2 == NUNIT // 2 - 1:
                lo = 512 * hc + 256 * jp
                nc.sync.dma_start(out=o_dram[:, :, lo:lo + 256], in_=dst)
            elif jp == 1:
                nc.sync.dma_start(out=o_dram[:, :, 512 * hc:512 * hc + 512],
                                  in_=ost[:].rearrange("p (b m) -> p b m", b=2))

        gather_unit(0)
        move_unit(0, nc.vector.tensor_copy)
        for hf in range(2):
            nc.vector.quantize_mx(out=xc[:, 512 * hf:512 * hf + 512].bitcast(FP8X4),
                                  scales=xs[:, 512 * hf:512 * hf + 512],
                                  in_=xgrp[:, 2048 * hf:2048 * hf + 2048])
        gather_unit(1)
        move_unit(1, nc.vector.tensor_copy)
        for u in range(NUNIT + 3):
            if u < NUNIT:
                transposes(u)
            if 2 <= u < NUNIT + 2:
                matmuls(u - 2)
            rotated_step = u >= 3 and PATTERN[(u - 3) // 2] == "R"
            add = finish(u - 3) if u >= 3 else None
            if u + 2 < NUNIT:
                gather_unit(u + 2)
            if 1 <= u < NUNIT + 1:
                quantise(u - 1)
            if u + 2 < NUNIT:
                on_scalar = u < 3 or (rotated_step and u % 2 == 0)
                move_unit(u + 2, nc.scalar.copy if on_scalar else nc.vector.tensor_copy)
            if add:
                add()
